import numpy as np
import ml_dtypes

BF16 = ml_dtypes.bfloat16


def bf(x):
    return np.asarray(x, np.float32).astype(BF16)


def f32(x):
    return np.asarray(x, np.float32)


def f64(x):
    return np.asarray(x).astype(np.float64)


def striped(idx):
    return np.tile(idx.reshape(-1, 16).T, (8, 1))


S, D, E, F, N = 2048, 128, 128, 384, 512


def setup_inputs():
    return {
        "table": bf(np.random.standard_normal((S, D))),
        "wn1": bf(np.random.standard_normal((D, E)) / np.sqrt(D)),
        "bn1": f32(0.1 * np.random.standard_normal((E, 1))),
        "wn2": bf(np.random.standard_normal((E, E)) * np.sqrt(2.0 / E)),
        "bn2": f32(0.1 * np.random.standard_normal((E, 1))),
        "anchor": bf(np.random.standard_normal((E, N))),
        "wp1": bf(np.random.standard_normal((F, E)) / np.sqrt(F)),
        "bp1": f32(0.1 * np.random.standard_normal((E, 1))),
        "offs": striped(np.random.permutation(np.tile(np.arange(S), 2))[:N]),
    }


def reference(table, wn1, bn1, wn2, bn2, anchor, wp1, bp1, offs):
    idx = offs[:16].T.reshape(-1)
    hid = np.maximum(f64(wn1).T @ f64(table)[idx].T + f64(bn1), 0.0)
    node = f64(wn2).T @ hid + f64(bn2)
    anc = f64(anchor)
    pair = np.concatenate([node, anc, node * anc], axis=0)
    return np.maximum(f64(wp1).T @ pair + f64(bp1), 0.0)

@@ -1,0 +1,81 @@
+import concourse.mybir as mybir
+from concourse.masks import make_identity
+
+NODES, FEATURES, UNITS, PAIRS = 2048, 128, 128, 512
+PAIR_BLOCKS = 3
+FLOPS = 2 * PAIRS * UNITS * (FEATURES + UNITS + PAIR_BLOCKS * UNITS)
+
+BF16, F32, U16 = mybir.dt.bfloat16, mybir.dt.float32, mybir.dt.uint16
+RELU, IDENTITY = mybir.ActivationFunctionType.Relu, mybir.ActivationFunctionType.Identity
+ADD, MULT, MAX = mybir.AluOpType.add, mybir.AluOpType.mult, mybir.AluOpType.max
+
+BLOCK = 128
+CHUNK_BLOCKS = 4
+CHUNK = CHUNK_BLOCKS * BLOCK
+CHUNKS = NODES // CHUNK
+
+
+def tile_pairactornetwork_kernel(tc, table, wn1, bn1, wn2, bn2, anchor, wp1, bp1, offs, out):
+    nc = tc.nc
+    with (
+        tc.tile_pool(name="held", bufs=1) as held,
+        tc.psum_pool(name="flip", bufs=CHUNKS) as flip,
+        tc.psum_pool(name="psum", bufs=1) as psum,
+    ):
+        offsets = held.tile([128, PAIRS // 16], U16, name="offsets")
+        nc.sync.dma_start(offsets[:], offs)
+
+        table_chunks = table.rearrange("(c b p) d -> c p b d", b=CHUNK_BLOCKS, p=BLOCK)
+        rows = []
+        for c in range(CHUNKS):
+            rows.append(held.tile([BLOCK, CHUNK_BLOCKS, FEATURES], BF16, name=f"rows{c}"))
+            queue = nc.sync if c % 2 == 0 else nc.scalar
+            queue.dma_start(rows[c][:], table_chunks[c])
+
+        identity = held.tile([BLOCK, BLOCK], BF16, name="identity")
+        make_identity(nc, identity[:])
+
+        wn1_sb = held.tile([FEATURES, UNITS], BF16, name="wn1_sb")
+        nc.sync.dma_start(wn1_sb[:], wn1)
+        bn1_sb = held.tile([UNITS, 1], F32, name="bn1_sb")
+        nc.sync.dma_start(bn1_sb[:], bn1)
+        wn2_sb = held.tile([UNITS, UNITS], BF16, name="wn2_sb")
+        nc.sync.dma_start(wn2_sb[:], wn2)
+        bn2_sb = held.tile([UNITS, 1], F32, name="bn2_sb")
+        nc.sync.dma_start(bn2_sb[:], bn2)
+        anchor_sb = held.tile([UNITS, PAIRS], BF16, name="anchor_sb")
+        nc.scalar.dma_start(anchor_sb[:], anchor)
+        wp1_sb = held.tile([UNITS, PAIR_BLOCKS, UNITS], BF16, name="wp1_sb")
+        nc.scalar.dma_start(wp1_sb[:], wp1.rearrange("(b f) m -> f b m", b=PAIR_BLOCKS))
+        bp1_sb = held.tile([UNITS, 1], F32, name="bp1_sb")
+        nc.scalar.dma_start(bp1_sb[:], bp1)
+
+        nodes_t = held.tile([FEATURES, NODES], BF16, name="nodes_t")
+        for c in range(CHUNKS):
+            flipped = flip.tile([FEATURES, CHUNK], BF16, name="flipped")
+            for b in range(CHUNK_BLOCKS):
+                nc.tensor.transpose(flipped[:, b * BLOCK : (b + 1) * BLOCK], rows[c][:, b, :], identity[:])
+            if c % 2 == 0:
+                nc.vector.tensor_copy(nodes_t[:, c * CHUNK : (c + 1) * CHUNK], flipped[:])
+            else:
+                nc.scalar.copy(nodes_t[:, c * CHUNK : (c + 1) * CHUNK], flipped[:])
+
+        hid_ps = psum.tile([UNITS, PAIRS], F32, name="hid_ps")
+        nc.tensor.matmul(hid_ps[:], wn1_sb[:], nodes_t[:].indirect(offsets[:]), start=True, stop=True)
+        hid = held.tile([UNITS, PAIRS], BF16, name="hid")
+        nc.scalar.activation(hid[:], hid_ps[:], RELU, bias=bn1_sb[:, 0:1])
+
+        node_ps = psum.tile([UNITS, PAIRS], F32, name="node_ps")
+        nc.tensor.matmul(node_ps[:], wn2_sb[:], hid[:], start=True, stop=True)
+        node = held.tile([UNITS, PAIRS], BF16, name="node")
+        nc.vector.tensor_scalar(node[:], node_ps[:], bn2_sb[:, 0:1], None, ADD)
+        product = held.tile([UNITS, PAIRS], BF16, name="product")
+        nc.vector.scalar_tensor_tensor(product[:], node_ps[:], bn2_sb[:, 0:1], anchor_sb[:], ADD, MULT)
+
+        out_ps = psum.tile([UNITS, PAIRS], F32, name="out_ps")
+        nc.tensor.matmul(out_ps[:], wp1_sb[:, 1, :], anchor_sb[:], start=True, stop=False)
+        nc.tensor.matmul(out_ps[:], wp1_sb[:, 0, :], node[:], start=False, stop=False)
+        nc.tensor.matmul(out_ps[:], wp1_sb[:, 2, :], product[:], start=False, stop=True)
+        out_sb = held.tile([UNITS, PAIRS], F32, name="out_sb")
+        nc.scalar.activation(out_sb[:], out_ps[:], RELU, bias=bp1_sb[:, 0:1])
+        nc.sync.dma_start(out, out_sb[:])

@@ -6,8 +6,8 @@ PAIR_BLOCKS = 3
 FLOPS = 2 * PAIRS * UNITS * (FEATURES + UNITS + PAIR_BLOCKS * UNITS)
 
 BF16, F32, U16 = mybir.dt.bfloat16, mybir.dt.float32, mybir.dt.uint16
-RELU, IDENTITY = mybir.ActivationFunctionType.Relu, mybir.ActivationFunctionType.Identity
-ADD, MULT, MAX = mybir.AluOpType.add, mybir.AluOpType.mult, mybir.AluOpType.max
+RELU = mybir.ActivationFunctionType.Relu
+ADD, MULT = mybir.AluOpType.add, mybir.AluOpType.mult
 
 BLOCK = 128
 CHUNK_BLOCKS = 4
@@ -19,13 +19,12 @@ def tile_pairactornetwork_kernel(tc, table, wn1, bn1, wn2, bn2, anchor, wp1, bp1
     nc = tc.nc
     with (
         tc.tile_pool(name="held", bufs=1) as held,
-        tc.psum_pool(name="flip", bufs=CHUNKS) as flip,
-        tc.psum_pool(name="psum", bufs=1) as psum,
+        tc.psum_pool(name="acc", bufs=1) as acc,
     ):
         offsets = held.tile([128, PAIRS // 16], U16, name="offsets")
         nc.sync.dma_start(offsets[:], offs)
 
-        table_chunks = table.rearrange("(c b p) d -> c p b d", b=CHUNK_BLOCKS, p=BLOCK)
+        table_chunks = table.rearrange("(c p b) d -> c p b d", p=BLOCK, b=CHUNK_BLOCKS)
         rows = []
         for c in range(CHUNKS):
             rows.append(held.tile([BLOCK, CHUNK_BLOCKS, FEATURES], BF16, name=f"rows{c}"))
@@ -51,28 +50,31 @@ def tile_pairactornetwork_kernel(tc, table, wn1, bn1, wn2, bn2, anchor, wp1, bp1
         nc.scalar.dma_start(bp1_sb[:], bp1)
 
         nodes_t = held.tile([FEATURES, NODES], BF16, name="nodes_t")
-        for c in range(CHUNKS):
-            flipped = flip.tile([FEATURES, CHUNK], BF16, name="flipped")
-            for b in range(CHUNK_BLOCKS):
-                nc.tensor.transpose(flipped[:, b * BLOCK : (b + 1) * BLOCK], rows[c][:, b, :], identity[:])
-            if c % 2 == 0:
-                nc.vector.tensor_copy(nodes_t[:, c * CHUNK : (c + 1) * CHUNK], flipped[:])
-            else:
-                nc.scalar.copy(nodes_t[:, c * CHUNK : (c + 1) * CHUNK], flipped[:])
+        with tc.psum_pool(name="flip", bufs=CHUNKS) as flip:
+            for c in range(CHUNKS):
+                flipped = flip.tile([FEATURES, CHUNK], BF16, name="flipped")
+                for b in range(CHUNK_BLOCKS):
+                    nc.tensor.transpose(flipped[:, b * BLOCK : (b + 1) * BLOCK], rows[c][:, b, :], identity[:])
+                in_order = flipped[:].rearrange("d (b p) -> d p b", b=CHUNK_BLOCKS)
+                window_part = nodes_t[:, c * CHUNK : (c + 1) * CHUNK].rearrange("d (p b) -> d p b", b=CHUNK_BLOCKS)
+                if c % 2 == 0:
+                    nc.vector.tensor_copy(window_part, in_order)
+                else:
+                    nc.scalar.copy(window_part, in_order)
 
-        hid_ps = psum.tile([UNITS, PAIRS], F32, name="hid_ps")
+        hid_ps = acc.tile([UNITS, PAIRS], F32, name="hid_ps")
         nc.tensor.matmul(hid_ps[:], wn1_sb[:], nodes_t[:].indirect(offsets[:]), start=True, stop=True)
         hid = held.tile([UNITS, PAIRS], BF16, name="hid")
         nc.scalar.activation(hid[:], hid_ps[:], RELU, bias=bn1_sb[:, 0:1])
 
-        node_ps = psum.tile([UNITS, PAIRS], F32, name="node_ps")
+        node_ps = acc.tile([UNITS, PAIRS], F32, name="node_ps")
         nc.tensor.matmul(node_ps[:], wn2_sb[:], hid[:], start=True, stop=True)
         node = held.tile([UNITS, PAIRS], BF16, name="node")
         nc.vector.tensor_scalar(node[:], node_ps[:], bn2_sb[:, 0:1], None, ADD)
         product = held.tile([UNITS, PAIRS], BF16, name="product")
         nc.vector.scalar_tensor_tensor(product[:], node_ps[:], bn2_sb[:, 0:1], anchor_sb[:], ADD, MULT)
 
-        out_ps = psum.tile([UNITS, PAIRS], F32, name="out_ps")
+        out_ps = acc.tile([UNITS, PAIRS], F32, name="out_ps")
         nc.tensor.matmul(out_ps[:], wp1_sb[:, 1, :], anchor_sb[:], start=True, stop=False)
         nc.tensor.matmul(out_ps[:], wp1_sb[:, 0, :], node[:], start=False, stop=False)
         nc.tensor.matmul(out_ps[:], wp1_sb[:, 2, :], product[:], start=False, stop=True)

@@ -6,13 +6,15 @@ PAIR_BLOCKS = 3
 FLOPS = 2 * PAIRS * UNITS * (FEATURES + UNITS + PAIR_BLOCKS * UNITS)
 
 BF16, F32, U16 = mybir.dt.bfloat16, mybir.dt.float32, mybir.dt.uint16
-RELU = mybir.ActivationFunctionType.Relu
-ADD, MULT = mybir.AluOpType.add, mybir.AluOpType.mult
+RELU, IDENTITY = mybir.ActivationFunctionType.Relu, mybir.ActivationFunctionType.Identity
+ADD, MULT, MAX = mybir.AluOpType.add, mybir.AluOpType.mult, mybir.AluOpType.max
 
 BLOCK = 128
 CHUNK_BLOCKS = 4
 CHUNK = CHUNK_BLOCKS * BLOCK
 CHUNKS = NODES // CHUNK
+HALVES = 2
+HALF = PAIRS // HALVES
 
 
 def tile_pairactornetwork_kernel(tc, table, wn1, bn1, wn2, bn2, anchor, wp1, bp1, offs, out):
@@ -24,7 +26,7 @@ def tile_pairactornetwork_kernel(tc, table, wn1, bn1, wn2, bn2, anchor, wp1, bp1
         offsets = held.tile([128, PAIRS // 16], U16, name="offsets")
         nc.sync.dma_start(offsets[:], offs)
 
-        table_chunks = table.rearrange("(c p b) d -> c p b d", p=BLOCK, b=CHUNK_BLOCKS)
+        table_chunks = table.rearrange("(c b p) d -> c p b d", b=CHUNK_BLOCKS, p=BLOCK)
         rows = []
         for c in range(CHUNKS):
             rows.append(held.tile([BLOCK, CHUNK_BLOCKS, FEATURES], BF16, name=f"rows{c}"))
@@ -55,29 +57,43 @@ def tile_pairactornetwork_kernel(tc, table, wn1, bn1, wn2, bn2, anchor, wp1, bp1
                 flipped = flip.tile([FEATURES, CHUNK], BF16, name="flipped")
                 for b in range(CHUNK_BLOCKS):
                     nc.tensor.transpose(flipped[:, b * BLOCK : (b + 1) * BLOCK], rows[c][:, b, :], identity[:])
-                in_order = flipped[:].rearrange("d (b p) -> d p b", b=CHUNK_BLOCKS)
-                window_part = nodes_t[:, c * CHUNK : (c + 1) * CHUNK].rearrange("d (p b) -> d p b", b=CHUNK_BLOCKS)
                 if c % 2 == 0:
-                    nc.vector.tensor_copy(window_part, in_order)
+                    nc.vector.tensor_copy(nodes_t[:, c * CHUNK : (c + 1) * CHUNK], flipped[:])
                 else:
-                    nc.scalar.copy(window_part, in_order)
+                    nc.scalar.copy(nodes_t[:, c * CHUNK : (c + 1) * CHUNK], flipped[:])
 
-        hid_ps = acc.tile([UNITS, PAIRS], F32, name="hid_ps")
-        nc.tensor.matmul(hid_ps[:], wn1_sb[:], nodes_t[:].indirect(offsets[:]), start=True, stop=True)
+        halves = [slice(h * HALF, (h + 1) * HALF) for h in range(HALVES)]
+
+        out_ps = [acc.tile([UNITS, HALF], F32, name=f"out_ps{h}") for h in range(HALVES)]
+        for h in range(HALVES):
+            nc.tensor.matmul(out_ps[h][:], wp1_sb[:, 1, :], anchor_sb[:, halves[h]], start=True, stop=False)
+
+        hid_ps = [acc.tile([UNITS, HALF], F32, name=f"hid_ps{h}") for h in range(HALVES)]
+        for h in range(HALVES):
+            picked = nodes_t[:].indirect(offsets[:, h * (HALF // 16) : (h + 1) * (HALF // 16)])
+            nc.tensor.matmul(hid_ps[h][:], wn1_sb[:], picked, start=True, stop=True)
         hid = held.tile([UNITS, PAIRS], BF16, name="hid")
-        nc.scalar.activation(hid[:], hid_ps[:], RELU, bias=bn1_sb[:, 0:1])
+        nc.scalar.activation(hid[:, halves[0]], hid_ps[0][:], RELU, bias=bn1_sb[:, 0:1])
+        nc.vector.tensor_scalar(hid[:, halves[1]], hid_ps[1][:], bn1_sb[:, 0:1], 0.0, ADD, MAX)
 
-        node_ps = acc.tile([UNITS, PAIRS], F32, name="node_ps")
-        nc.tensor.matmul(node_ps[:], wn2_sb[:], hid[:], start=True, stop=True)
         node = held.tile([UNITS, PAIRS], BF16, name="node")
-        nc.vector.tensor_scalar(node[:], node_ps[:], bn2_sb[:, 0:1], None, ADD)
         product = held.tile([UNITS, PAIRS], BF16, name="product")
-        nc.vector.scalar_tensor_tensor(product[:], node_ps[:], bn2_sb[:, 0:1], anchor_sb[:], ADD, MULT)
+        with tc.psum_pool(name="twice", bufs=1) as twice:
+            for h in range(HALVES):
+                for_node = twice.tile([UNITS, HALF], F32, name=f"for_node{h}")
+                nc.tensor.matmul(for_node[:], wn2_sb[:], hid[:, halves[h]], start=True, stop=True)
+                for_product = twice.tile([UNITS, HALF], F32, name=f"for_product{h}")
+                nc.tensor.matmul(for_product[:], wn2_sb[:], hid[:, halves[h]], start=True, stop=True)
+                nc.scalar.activation(node[:, halves[h]], for_node[:], IDENTITY, bias=bn2_sb[:, 0:1])
+                nc.vector.scalar_tensor_tensor(
+                    product[:, halves[h]], for_product[:], bn2_sb[:, 0:1], anchor_sb[:, halves[h]], ADD, MULT
+                )
 
-        out_ps = acc.tile([UNITS, PAIRS], F32, name="out_ps")
-        nc.tensor.matmul(out_ps[:], wp1_sb[:, 1, :], anchor_sb[:], start=True, stop=False)
-        nc.tensor.matmul(out_ps[:], wp1_sb[:, 0, :], node[:], start=False, stop=False)
-        nc.tensor.matmul(out_ps[:], wp1_sb[:, 2, :], product[:], start=False, stop=True)
-        out_sb = held.tile([UNITS, PAIRS], F32, name="out_sb")
-        nc.scalar.activation(out_sb[:], out_ps[:], RELU, bias=bp1_sb[:, 0:1])
-        nc.sync.dma_start(out, out_sb[:])
+        for h in range(HALVES):
+            nc.tensor.matmul(out_ps[h][:], wp1_sb[:, 0, :], node[:, halves[h]], start=False, stop=False)
+            nc.tensor.matmul(out_ps[h][:], wp1_sb[:, 2, :], product[:, halves[h]], start=False, stop=True)
+        out_sb = [held.tile([UNITS, HALF], F32, name=f"out_sb{h}") for h in range(HALVES)]
+        nc.scalar.activation(out_sb[0][:], out_ps[0][:], RELU, bias=bp1_sb[:, 0:1])
+        nc.sync.dma_start(out[:, halves[0]], out_sb[0][:])
+        nc.vector.tensor_scalar(out_sb[1][:], out_ps[1][:], bp1_sb[:, 0:1], 0.0, ADD, MAX)
+        nc.scalar.dma_start(out[:, halves[1]], out_sb[1][:])

@@ -13,6 +13,8 @@ BLOCK = 128
 CHUNK_BLOCKS = 4
 CHUNK = CHUNK_BLOCKS * BLOCK
 CHUNKS = NODES // CHUNK
+FLIP_BANKS = 3
+WARM_UP = 6
 HALVES = 2
 HALF = PAIRS // HALVES
 
@@ -26,7 +28,7 @@ def tile_pairactornetwork_kernel(tc, table, wn1, bn1, wn2, bn2, anchor, wp1, bp1
         offsets = held.tile([128, PAIRS // 16], U16, name="offsets")
         nc.sync.dma_start(offsets[:], offs)
 
-        table_chunks = table.rearrange("(c b p) d -> c p b d", b=CHUNK_BLOCKS, p=BLOCK)
+        table_chunks = table.rearrange("(c p b) d -> c p b d", p=BLOCK, b=CHUNK_BLOCKS)
         rows = []
         for c in range(CHUNKS):
             rows.append(held.tile([BLOCK, CHUNK_BLOCKS, FEATURES], BF16, name=f"rows{c}"))
@@ -51,16 +53,29 @@ def tile_pairactornetwork_kernel(tc, table, wn1, bn1, wn2, bn2, anchor, wp1, bp1
         bp1_sb = held.tile([UNITS, 1], F32, name="bp1_sb")
         nc.scalar.dma_start(bp1_sb[:], bp1)
 
+        idle_in = held.tile([BLOCK, PAIRS], BF16, name="idle_in")
+        nc.vector.memset(idle_in[:], 0.0)
+
         nodes_t = held.tile([FEATURES, NODES], BF16, name="nodes_t")
-        with tc.psum_pool(name="flip", bufs=CHUNKS) as flip:
+        with (
+            tc.psum_pool(name="idle", bufs=1) as idle,
+            tc.psum_pool(name="flip", bufs=FLIP_BANKS) as flip,
+        ):
+            idle_ps = idle.tile([BLOCK, PAIRS], F32, name="idle_ps")
+            for i in range(WARM_UP):
+                nc.tensor.matmul(idle_ps[:], idle_in[:, 0:BLOCK], idle_in[:], start=True, stop=True)
             for c in range(CHUNKS):
+                if c > 0:
+                    nc.tensor.matmul(idle_ps[:, 0:HALF], idle_in[:, 0:BLOCK], idle_in[:, 0:HALF], start=True, stop=True)
                 flipped = flip.tile([FEATURES, CHUNK], BF16, name="flipped")
                 for b in range(CHUNK_BLOCKS):
                     nc.tensor.transpose(flipped[:, b * BLOCK : (b + 1) * BLOCK], rows[c][:, b, :], identity[:])
+                in_order = flipped[:].rearrange("d (b p) -> d p b", b=CHUNK_BLOCKS)
+                window_part = nodes_t[:, c * CHUNK : (c + 1) * CHUNK].rearrange("d (p b) -> d p b", b=CHUNK_BLOCKS)
                 if c % 2 == 0:
-                    nc.vector.tensor_copy(nodes_t[:, c * CHUNK : (c + 1) * CHUNK], flipped[:])
+                    nc.vector.tensor_copy(window_part, in_order)
                 else:
-                    nc.scalar.copy(nodes_t[:, c * CHUNK : (c + 1) * CHUNK], flipped[:])
+                    nc.scalar.copy(window_part, in_order)
 
         halves = [slice(h * HALF, (h + 1) * HALF) for h in range(HALVES)]
 

@@ -13,8 +13,6 @@ BLOCK = 128
 CHUNK_BLOCKS = 4
 CHUNK = CHUNK_BLOCKS * BLOCK
 CHUNKS = NODES // CHUNK
-FLIP_BANKS = 3
-WARM_UP = 6
 HALVES = 2
 HALF = PAIRS // HALVES
 
@@ -53,20 +51,9 @@ def tile_pairactornetwork_kernel(tc, table, wn1, bn1, wn2, bn2, anchor, wp1, bp1
         bp1_sb = held.tile([UNITS, 1], F32, name="bp1_sb")
         nc.scalar.dma_start(bp1_sb[:], bp1)
 
-        idle_in = held.tile([BLOCK, PAIRS], BF16, name="idle_in")
-        nc.vector.memset(idle_in[:], 0.0)
-
         nodes_t = held.tile([FEATURES, NODES], BF16, name="nodes_t")
-        with (
-            tc.psum_pool(name="idle", bufs=1) as idle,
-            tc.psum_pool(name="flip", bufs=FLIP_BANKS) as flip,
-        ):
-            idle_ps = idle.tile([BLOCK, PAIRS], F32, name="idle_ps")
-            for i in range(WARM_UP):
-                nc.tensor.matmul(idle_ps[:], idle_in[:, 0:BLOCK], idle_in[:], start=True, stop=True)
+        with tc.psum_pool(name="flip", bufs=CHUNKS) as flip:
             for c in range(CHUNKS):
-                if c > 0:
-                    nc.tensor.matmul(idle_ps[:, 0:HALF], idle_in[:, 0:BLOCK], idle_in[:, 0:HALF], start=True, stop=True)
                 flipped = flip.tile([FEATURES, CHUNK], BF16, name="flipped")
                 for b in range(CHUNK_BLOCKS):
                     nc.tensor.transpose(flipped[:, b * BLOCK : (b + 1) * BLOCK], rows[c][:, b, :], identity[:])

@@ -13,6 +13,8 @@ BLOCK = 128
 CHUNK_BLOCKS = 4
 CHUNK = CHUNK_BLOCKS * BLOCK
 CHUNKS = NODES // CHUNK
+FLIP_BANKS = 3
+WARM_UP = 9
 HALVES = 2
 HALF = PAIRS // HALVES
 
@@ -51,9 +53,20 @@ def tile_pairactornetwork_kernel(tc, table, wn1, bn1, wn2, bn2, anchor, wp1, bp1
         bp1_sb = held.tile([UNITS, 1], F32, name="bp1_sb")
         nc.scalar.dma_start(bp1_sb[:], bp1)
 
+        idle_in = held.tile([BLOCK, PAIRS], BF16, name="idle_in")
+        nc.vector.memset(idle_in[:], 0.0)
+
         nodes_t = held.tile([FEATURES, NODES], BF16, name="nodes_t")
-        with tc.psum_pool(name="flip", bufs=CHUNKS) as flip:
+        with (
+            tc.psum_pool(name="idle", bufs=1) as idle,
+            tc.psum_pool(name="flip", bufs=FLIP_BANKS) as flip,
+        ):
+            idle_ps = idle.tile([BLOCK, PAIRS], F32, name="idle_ps")
+            for i in range(WARM_UP):
+                nc.tensor.matmul(idle_ps[:], idle_in[:, 0:BLOCK], idle_in[:], start=True, stop=True)
             for c in range(CHUNKS):
+                if c > 0:
+                    nc.tensor.matmul(idle_ps[:, 0:HALF], idle_in[:, 0:BLOCK], idle_in[:, 0:HALF], start=True, stop=True)
                 flipped = flip.tile([FEATURES, CHUNK], BF16, name="flipped")
                 for b in range(CHUNK_BLOCKS):
                     nc.tensor.transpose(flipped[:, b * BLOCK : (b + 1) * BLOCK], rows[c][:, b, :], identity[:])

@@ -14,7 +14,7 @@ CHUNK_BLOCKS = 4
 CHUNK = CHUNK_BLOCKS * BLOCK
 CHUNKS = NODES // CHUNK
 FLIP_BANKS = 3
-WARM_UP = 9
+WARM_UP = 5
 HALVES = 2
 HALF = PAIRS // HALVES
 
@@ -32,8 +32,7 @@ def tile_pairactornetwork_kernel(tc, table, wn1, bn1, wn2, bn2, anchor, wp1, bp1
         rows = []
         for c in range(CHUNKS):
             rows.append(held.tile([BLOCK, CHUNK_BLOCKS, FEATURES], BF16, name=f"rows{c}"))
-            queue = nc.sync if c % 2 == 0 else nc.scalar
-            queue.dma_start(rows[c][:], table_chunks[c])
+            nc.sync.dma_start(rows[c][:], table_chunks[c])
 
         identity = held.tile([BLOCK, BLOCK], BF16, name="identity")
         make_identity(nc, identity[:])
@@ -47,11 +46,11 @@ def tile_pairactornetwork_kernel(tc, table, wn1, bn1, wn2, bn2, anchor, wp1, bp1
         bn2_sb = held.tile([UNITS, 1], F32, name="bn2_sb")
         nc.sync.dma_start(bn2_sb[:], bn2)
         anchor_sb = held.tile([UNITS, PAIRS], BF16, name="anchor_sb")
-        nc.scalar.dma_start(anchor_sb[:], anchor)
+        nc.sync.dma_start(anchor_sb[:], anchor)
         wp1_sb = held.tile([UNITS, PAIR_BLOCKS, UNITS], BF16, name="wp1_sb")
-        nc.scalar.dma_start(wp1_sb[:], wp1.rearrange("(b f) m -> f b m", b=PAIR_BLOCKS))
+        nc.sync.dma_start(wp1_sb[:], wp1.rearrange("(b f) m -> f b m", b=PAIR_BLOCKS))
         bp1_sb = held.tile([UNITS, 1], F32, name="bp1_sb")
-        nc.scalar.dma_start(bp1_sb[:], bp1)
+        nc.sync.dma_start(bp1_sb[:], bp1)
 
         idle_in = held.tile([BLOCK, PAIRS], BF16, name="idle_in")
         nc.vector.memset(idle_in[:], 0.0)
@@ -76,12 +75,9 @@ def tile_pairactornetwork_kernel(tc, table, wn1, bn1, wn2, bn2, anchor, wp1, bp1
                     nc.vector.tensor_copy(window_part, in_order)
                 else:
                     nc.scalar.copy(window_part, in_order)
+            nc.tensor.matmul(idle_ps[:], idle_in[:, 0:BLOCK], idle_in[:], start=True, stop=True)
 
         halves = [slice(h * HALF, (h + 1) * HALF) for h in range(HALVES)]
-
-        out_ps = [acc.tile([UNITS, HALF], F32, name=f"out_ps{h}") for h in range(HALVES)]
-        for h in range(HALVES):
-            nc.tensor.matmul(out_ps[h][:], wp1_sb[:, 1, :], anchor_sb[:, halves[h]], start=True, stop=False)
 
         hid_ps = [acc.tile([UNITS, HALF], F32, name=f"hid_ps{h}") for h in range(HALVES)]
         for h in range(HALVES):
@@ -104,6 +100,9 @@ def tile_pairactornetwork_kernel(tc, table, wn1, bn1, wn2, bn2, anchor, wp1, bp1
                     product[:, halves[h]], for_product[:], bn2_sb[:, 0:1], anchor_sb[:, halves[h]], ADD, MULT
                 )
 
+        out_ps = [acc.tile([UNITS, HALF], F32, name=f"out_ps{h}") for h in range(HALVES)]
+        for h in range(HALVES):
+            nc.tensor.matmul(out_ps[h][:], wp1_sb[:, 1, :], anchor_sb[:, halves[h]], start=True, stop=False)
         for h in range(HALVES):
             nc.tensor.matmul(out_ps[h][:], wp1_sb[:, 0, :], node[:, halves[h]], start=False, stop=False)
             nc.tensor.matmul(out_ps[h][:], wp1_sb[:, 2, :], product[:, halves[h]], start=False, stop=True)

@@ -25,14 +25,15 @@ def tile_pairactornetwork_kernel(tc, table, wn1, bn1, wn2, bn2, anchor, wp1, bp1
         tc.tile_pool(name="held", bufs=1) as held,
         tc.psum_pool(name="acc", bufs=1) as acc,
     ):
-        offsets = held.tile([128, PAIRS // 16], U16, name="offsets")
-        nc.sync.dma_start(offsets[:], offs)
-
         table_chunks = table.rearrange("(c p b) d -> c p b d", p=BLOCK, b=CHUNK_BLOCKS)
         rows = []
         for c in range(CHUNKS):
             rows.append(held.tile([BLOCK, CHUNK_BLOCKS, FEATURES], BF16, name=f"rows{c}"))
-            nc.sync.dma_start(rows[c][:], table_chunks[c])
+            queue = nc.sync if c % 2 == 0 else nc.scalar
+            queue.dma_start(rows[c][:], table_chunks[c])
+
+        offsets = held.tile([128, PAIRS // 16], U16, name="offsets")
+        nc.sync.dma_start(offsets[:], offs)
 
         identity = held.tile([BLOCK, BLOCK], BF16, name="identity")
         make_identity(nc, identity[:])
@@ -46,11 +47,11 @@ def tile_pairactornetwork_kernel(tc, table, wn1, bn1, wn2, bn2, anchor, wp1, bp1
         bn2_sb = held.tile([UNITS, 1], F32, name="bn2_sb")
         nc.sync.dma_start(bn2_sb[:], bn2)
         anchor_sb = held.tile([UNITS, PAIRS], BF16, name="anchor_sb")
-        nc.sync.dma_start(anchor_sb[:], anchor)
+        nc.scalar.dma_start(anchor_sb[:], anchor)
         wp1_sb = held.tile([UNITS, PAIR_BLOCKS, UNITS], BF16, name="wp1_sb")
-        nc.sync.dma_start(wp1_sb[:], wp1.rearrange("(b f) m -> f b m", b=PAIR_BLOCKS))
+        nc.scalar.dma_start(wp1_sb[:], wp1.rearrange("(b f) m -> f b m", b=PAIR_BLOCKS))
         bp1_sb = held.tile([UNITS, 1], F32, name="bp1_sb")
-        nc.sync.dma_start(bp1_sb[:], bp1)
+        nc.scalar.dma_start(bp1_sb[:], bp1)
 
         idle_in = held.tile([BLOCK, PAIRS], BF16, name="idle_in")
         nc.vector.memset(idle_in[:], 0.0)
@@ -75,9 +76,12 @@ def tile_pairactornetwork_kernel(tc, table, wn1, bn1, wn2, bn2, anchor, wp1, bp1
                     nc.vector.tensor_copy(window_part, in_order)
                 else:
                     nc.scalar.copy(window_part, in_order)
-            nc.tensor.matmul(idle_ps[:], idle_in[:, 0:BLOCK], idle_in[:], start=True, stop=True)
 
         halves = [slice(h * HALF, (h + 1) * HALF) for h in range(HALVES)]
+
+        out_ps = [acc.tile([UNITS, HALF], F32, name=f"out_ps{h}") for h in range(HALVES)]
+        for h in range(HALVES):
+            nc.tensor.matmul(out_ps[h][:], wp1_sb[:, 1, :], anchor_sb[:, halves[h]], start=True, stop=False)
 
         hid_ps = [acc.tile([UNITS, HALF], F32, name=f"hid_ps{h}") for h in range(HALVES)]
         for h in range(HALVES):
@@ -100,9 +104,6 @@ def tile_pairactornetwork_kernel(tc, table, wn1, bn1, wn2, bn2, anchor, wp1, bp1
                     product[:, halves[h]], for_product[:], bn2_sb[:, 0:1], anchor_sb[:, halves[h]], ADD, MULT
                 )
 
-        out_ps = [acc.tile([UNITS, HALF], F32, name=f"out_ps{h}") for h in range(HALVES)]
-        for h in range(HALVES):
-            nc.tensor.matmul(out_ps[h][:], wp1_sb[:, 1, :], anchor_sb[:, halves[h]], start=True, stop=False)
         for h in range(HALVES):
             nc.tensor.matmul(out_ps[h][:], wp1_sb[:, 0, :], node[:, halves[h]], start=False, stop=False)
             nc.tensor.matmul(out_ps[h][:], wp1_sb[:, 2, :], product[:, halves[h]], start=False, stop=True)

import concourse.mybir as mybir
from concourse.masks import make_identity

NODES, FEATURES, UNITS, PAIRS = 2048, 128, 128, 512
PAIR_BLOCKS = 3
FLOPS = 2 * PAIRS * UNITS * (FEATURES + UNITS + PAIR_BLOCKS * UNITS)

BF16, F32, U16 = mybir.dt.bfloat16, mybir.dt.float32, mybir.dt.uint16
RELU, IDENTITY = mybir.ActivationFunctionType.Relu, mybir.ActivationFunctionType.Identity
ADD, MULT, MAX = mybir.AluOpType.add, mybir.AluOpType.mult, mybir.AluOpType.max

BLOCK = 128
CHUNK_BLOCKS = 4
CHUNK = CHUNK_BLOCKS * BLOCK
CHUNKS = NODES // CHUNK
FLIP_BANKS = 3
WARM_UP = 5
HALVES = 2
HALF = PAIRS // HALVES


def tile_pairactornetwork_kernel(tc, table, wn1, bn1, wn2, bn2, anchor, wp1, bp1, offs, out):
    nc = tc.nc
    with (
        tc.tile_pool(name="held", bufs=1) as held,
        tc.psum_pool(name="acc", bufs=1) as acc,
    ):
        table_chunks = table.rearrange("(c p b) d -> c p b d", p=BLOCK, b=CHUNK_BLOCKS)
        rows = []
        for c in range(CHUNKS):
            rows.append(held.tile([BLOCK, CHUNK_BLOCKS, FEATURES], BF16, name=f"rows{c}"))
            queue = nc.sync if c % 2 == 0 else nc.scalar
            queue.dma_start(rows[c][:], table_chunks[c])

        offsets = held.tile([128, PAIRS // 16], U16, name="offsets")
        nc.sync.dma_start(offsets[:], offs)

        identity = held.tile([BLOCK, BLOCK], BF16, name="identity")
        make_identity(nc, identity[:])

        wn1_sb = held.tile([FEATURES, UNITS], BF16, name="wn1_sb")
        nc.sync.dma_start(wn1_sb[:], wn1)
        bn1_sb = held.tile([UNITS, 1], F32, name="bn1_sb")
        nc.sync.dma_start(bn1_sb[:], bn1)
        wn2_sb = held.tile([UNITS, UNITS], BF16, name="wn2_sb")
        nc.sync.dma_start(wn2_sb[:], wn2)
        bn2_sb = held.tile([UNITS, 1], F32, name="bn2_sb")
        nc.sync.dma_start(bn2_sb[:], bn2)
        anchor_sb = held.tile([UNITS, PAIRS], BF16, name="anchor_sb")
        nc.scalar.dma_start(anchor_sb[:], anchor)
        wp1_sb = held.tile([UNITS, PAIR_BLOCKS, UNITS], BF16, name="wp1_sb")
        nc.scalar.dma_start(wp1_sb[:], wp1.rearrange("(b f) m -> f b m", b=PAIR_BLOCKS))
        bp1_sb = held.tile([UNITS, 1], F32, name="bp1_sb")
        nc.scalar.dma_start(bp1_sb[:], bp1)

        idle_in = held.tile([BLOCK, PAIRS], BF16, name="idle_in")
        nc.vector.memset(idle_in[:], 0.0)

        nodes_t = held.tile([FEATURES, NODES], BF16, name="nodes_t")
        with (
            tc.psum_pool(name="idle", bufs=1) as idle,
            tc.psum_pool(name="flip", bufs=FLIP_BANKS) as flip,
        ):
            idle_ps = idle.tile([BLOCK, PAIRS], F32, name="idle_ps")
            for i in range(WARM_UP):
                nc.tensor.matmul(idle_ps[:], idle_in[:, 0:BLOCK], idle_in[:], start=True, stop=True)
            for c in range(CHUNKS):
                if c > 0:
                    nc.tensor.matmul(idle_ps[:, 0:HALF], idle_in[:, 0:BLOCK], idle_in[:, 0:HALF], start=True, stop=True)
                flipped = flip.tile([FEATURES, CHUNK], BF16, name="flipped")
                for b in range(CHUNK_BLOCKS):
                    nc.tensor.transpose(flipped[:, b * BLOCK : (b + 1) * BLOCK], rows[c][:, b, :], identity[:])
                in_order = flipped[:].rearrange("d (b p) -> d p b", b=CHUNK_BLOCKS)
                window_part = nodes_t[:, c * CHUNK : (c + 1) * CHUNK].rearrange("d (p b) -> d p b", b=CHUNK_BLOCKS)
                if c % 2 == 0:
                    nc.vector.tensor_copy(window_part, in_order)
                else:
                    nc.scalar.copy(window_part, in_order)

        halves = [slice(h * HALF, (h + 1) * HALF) for h in range(HALVES)]

        out_ps = [acc.tile([UNITS, HALF], F32, name=f"out_ps{h}") for h in range(HALVES)]
        for h in range(HALVES):
            nc.tensor.matmul(out_ps[h][:], wp1_sb[:, 1, :], anchor_sb[:, halves[h]], start=True, stop=False)

        hid_ps = [acc.tile([UNITS, HALF], F32, name=f"hid_ps{h}") for h in range(HALVES)]
        for h in range(HALVES):
            picked = nodes_t[:].indirect(offsets[:, h * (HALF // 16) : (h + 1) * (HALF // 16)])
            nc.tensor.matmul(hid_ps[h][:], wn1_sb[:], picked, start=True, stop=True)
        hid = held.tile([UNITS, PAIRS], BF16, name="hid")
        nc.scalar.activation(hid[:, halves[0]], hid_ps[0][:], RELU, bias=bn1_sb[:, 0:1])
        nc.vector.tensor_scalar(hid[:, halves[1]], hid_ps[1][:], bn1_sb[:, 0:1], 0.0, ADD, MAX)

        node = held.tile([UNITS, PAIRS], BF16, name="node")
        product = held.tile([UNITS, PAIRS], BF16, name="product")
        with tc.psum_pool(name="twice", bufs=1) as twice:
            for h in range(HALVES):
                for_node = twice.tile([UNITS, HALF], F32, name=f"for_node{h}")
                nc.tensor.matmul(for_node[:], wn2_sb[:], hid[:, halves[h]], start=True, stop=True)
                for_product = twice.tile([UNITS, HALF], F32, name=f"for_product{h}")
                nc.tensor.matmul(for_product[:], wn2_sb[:], hid[:, halves[h]], start=True, stop=True)
                nc.scalar.activation(node[:, halves[h]], for_node[:], IDENTITY, bias=bn2_sb[:, 0:1])
                nc.vector.scalar_tensor_tensor(
                    product[:, halves[h]], for_product[:], bn2_sb[:, 0:1], anchor_sb[:, halves[h]], ADD, MULT
                )

        for h in range(HALVES):
            nc.tensor.matmul(out_ps[h][:], wp1_sb[:, 0, :], node[:, halves[h]], start=False, stop=False)
            nc.tensor.matmul(out_ps[h][:], wp1_sb[:, 2, :], product[:, halves[h]], start=False, stop=True)
        out_sb = [held.tile([UNITS, HALF], F32, name=f"out_sb{h}") for h in range(HALVES)]
        nc.scalar.activation(out_sb[0][:], out_ps[0][:], RELU, bias=bp1_sb[:, 0:1])
        nc.sync.dma_start(out[:, halves[0]], out_sb[0][:])
        nc.vector.tensor_scalar(out_sb[1][:], out_ps[1][:], bp1_sb[:, 0:1], 0.0, ADD, MAX)
        nc.scalar.dma_start(out[:, halves[1]], out_sb[1][:])
